import numpy as np
import ml_dtypes


def mxq(x, axis, fmt="e4m3"):
    dtype, down = {"e4m3": (ml_dtypes.float8_e4m3fn, 7), "e5m2": (ml_dtypes.float8_e5m2, 14)}[fmt]
    v = np.moveaxis(np.asarray(x, np.float32).astype(ml_dtypes.bfloat16).astype(np.float64), axis, -1)
    blocks = v.reshape(v.shape[:-1] + (-1, 32))
    amax = np.abs(blocks).max(-1, keepdims=True)
    byte = np.maximum(np.where(amax > 0, np.frexp(amax)[1] - 1 + 127, 0) - down, 1)
    scale = np.exp2(byte - 127.0)
    codes = (blocks / scale).astype(np.float32).astype(dtype).astype(np.float64)
    return np.moveaxis((codes * scale).reshape(v.shape), -1, axis)


WIDE = False


def mx_kscale(k):
    if not WIDE:
        return np.ones(k)
    levels = np.array([10, -10, 5, -5, 0])
    a = np.random.permutation(np.resize(levels, k // 512 * 4)).reshape(k // 512, 4)
    idx = np.arange(k)
    return np.exp2(a[idx // 512, idx % 128 // 32])


BF16 = ml_dtypes.bfloat16


def bf(x):
    return np.asarray(x, np.float32).astype(BF16)


def f64(x):
    return np.asarray(x).astype(np.float64)


B, S, D, R, O = 2, 1024, 1024, 1024, 1024


def rfs(xw, dot_products, ab, AB):
    correction = (0.5 * np.sum(xw * xw, axis=-1))[..., None] * (ab * ab)
    return (1.0 / np.sqrt(R)) * AB * np.exp(dot_products - correction)


def setup_inputs():
    s = mx_kscale(D)
    s = s / s.max()
    return {"x": bf(np.random.standard_normal((B, S, D)) * 2.0 / np.sqrt(D) * s),
            "input_weights": bf(np.random.standard_normal((O, D)) * 2.0 / np.sqrt(D) * s),
            "xis": bf(np.random.uniform(size=R) * 0.5),
            "proj_matrix": bf(np.random.standard_normal((R, D)) / s)}


def reference(x, input_weights, xis, proj_matrix):
    x, input_weights, xis, proj_matrix = f64(x), f64(input_weights), f64(xis), f64(proj_matrix)
    ab = xis
    AB = np.exp(xis)
    gq = mxq(ab[:, None] * proj_matrix, 1, "e4m3")
    weights = rfs(input_weights, mxq(input_weights, 1, "e4m3") @ gq.T, ab, AB)
    feats = rfs(x, mxq(x, 2, "e4m3") @ gq.T, ab, AB)
    return mxq(feats, 2, "e4m3") @ mxq(weights, 1, "e4m3").T

@@ -1,0 +1,428 @@
+import math
+from contextlib import ExitStack
+
+import concourse.mybir as mybir
+from concourse.masks import make_identity
+
+F32 = mybir.dt.float32
+BF16 = mybir.dt.bfloat16
+U32 = mybir.dt.uint32
+U8 = mybir.dt.uint8
+FP8X4 = mybir.dt.float8_e4m3fn_x4
+ALU = mybir.AluOpType
+ACT = mybir.ActivationFunctionType
+
+P = 128
+PACK = 4
+D = 1024
+R = 1024
+O = 1024
+T = 2048
+CHUNK = 512
+ROWS = CHUNK // P
+PASSES = 2
+W_CHUNKS = O // CHUNK
+CHUNKS = W_CHUNKS + T // CHUNK
+PER_CHUNK = PASSES * PACK
+
+FLOPS = 2 * (O * D * R + T * D * R + T * R * O)
+
+BANKS = 8
+S1_BANKS = (0, 1, 2)
+S2_BANKS = (3, 4, 5)
+T_BANKS = (6, 7)
+
+WARM_UP = 4
+LEAD = 2
+EXP_LAG = 2
+QUANT_LAG = 3
+S2_FIRST = 3 * PER_CHUNK + EXP_LAG + QUANT_LAG
+
+
+def tile_nnk_kernel(tc, x, input_weights, xis, proj_matrix, out):
+    nc = tc.nc
+    x_rows = x.flatten_outer_dims()
+    out_rows = out.flatten_outer_dims()
+
+    with ExitStack() as ctx:
+        ctx.enter_context(tc.manual_schedule())
+        const = ctx.enter_context(tc.tile_pool(name="const", bufs=1))
+        raws = ctx.enter_context(tc.tile_pool(name="raws", bufs=1))
+        keep = ctx.enter_context(tc.tile_pool(name="keep", bufs=1))
+        work = ctx.enter_context(tc.tile_pool(name="work", bufs=2))
+        psum = ctx.enter_context(tc.psum_pool(name="psum", bufs=1))
+
+        live = {}
+
+        def bank(b):
+            return psum.tile([P, CHUNK], F32, name="bank%d" % b)
+
+        queued = {"V": 0, "S": 0}
+
+        def count(eng, elements):
+            queued[eng] = queued[eng] + elements
+
+        def idler():
+            return "V" if queued["V"] <= queued["S"] else "S"
+
+        def copy_out(dst, src):
+            eng = idler()
+            count(eng, CHUNK)
+            if eng == "V":
+                nc.vector.tensor_copy(out=dst, in_=src)
+            else:
+                nc.scalar.copy(out=dst, in_=src)
+
+        xis_bf = const.tile([P, PASSES, PACK], BF16, name="xis_bf")
+        nc.sync.dma_start(out=xis_bf[:], in_=xis.rearrange("(c p j) -> p c j", c=PASSES, p=P, j=PACK))
+        proj_raw = []
+        chunk_raw = []
+
+        def load_proj(c, pieces):
+            raw = raws.tile([P, PACK * D], BF16, name="proj_raw%d" % c)
+            src = proj_matrix[c * CHUNK : (c + 1) * CHUNK, :].rearrange("(p j) d -> p j d", j=PACK)
+            dst = raw[:].rearrange("p (j d) -> p j d", j=PACK)
+            rows = PACK // pieces
+            for j in range(0, PACK, rows):
+                nc.sync.dma_start(out=dst[:, j : j + rows, :], in_=src[:, j : j + rows, :])
+            proj_raw.append(raw)
+
+        def load_chunk(k):
+            raw = raws.tile([P, ROWS * D], BF16, name="chunk_raw%d" % k)
+            if k < W_CHUNKS:
+                src = input_weights[k * CHUNK : (k + 1) * CHUNK, :].rearrange("(n p) d -> p n d", p=P)
+            else:
+                m = k - W_CHUNKS
+                src = x_rows[m * CHUNK : (m + 1) * CHUNK, :].rearrange("(p n) d -> p n d", n=ROWS)
+            nc.sync.dma_start(out=raw[:].rearrange("p (n d) -> p n d", n=ROWS), in_=src)
+            chunk_raw.append(raw)
+
+        load_proj(0, PACK)
+        load_chunk(0)
+        load_proj(1, 1)
+        for k in range(1, CHUNKS):
+            load_chunk(k)
+
+        ident = const.tile([P, P], F32, name="ident")
+        make_identity(nc, ident[:])
+        warm = const.tile([P, 1], F32, name="warm")
+        nc.vector.memset(warm[:], 0.0)
+        nc.scalar.activation(out=warm[:], in_=warm[:], func=ACT.Exp)
+        zeros = const.tile([P, CHUNK], BF16, name="zeros")
+        nc.vector.memset(zeros[:], 0.0)
+        idle = bank(BANKS - 1)
+        for rep in range(WARM_UP):
+            nc.tensor.matmul(out=idle[:], lhsT=zeros[:, 0:P], rhs=zeros[:], start=True, stop=True)
+        xis32 = const.tile([P, PER_CHUNK], F32, name="xis32")
+        nc.vector.tensor_copy(out=xis32[:], in_=xis_bf[:].rearrange("p c j -> p (c j)"))
+        diag = const.tile([P, PER_CHUNK, P], BF16, name="diag")
+        for cj in range(PER_CHUNK):
+            nc.vector.tensor_scalar_mul(out=diag[:, cj, :], in0=ident[:], scalar1=xis32[:, cj : cj + 1])
+        neg_half_sq = const.tile([P, PER_CHUNK], F32, name="neg_half_sq")
+        nc.vector.scalar_tensor_tensor(
+            out=neg_half_sq[:], in0=xis32[:], scalar=-0.5, in1=xis32[:], op0=ALU.mult, op1=ALU.mult
+        )
+        exp_bias = const.tile([P, PER_CHUNK], F32, name="exp_bias")
+        nc.vector.tensor_scalar_add(out=exp_bias[:], in0=xis32[:], scalar1=-math.log(32.0))
+
+        g_grouped = keep.tile([P, PASSES * PASSES * CHUNK * PACK], BF16, name="g_grouped", align_bytes=64)
+        g_codes = keep.tile([P, PASSES * PASSES * CHUNK], U32, name="g_codes", align_bytes=64)
+        g_scales = keep.tile([P, PASSES * PASSES * CHUNK], U8, name="g_scales", align_bytes=64)
+        w_codes = keep.tile([P, PASSES * O], U32, name="w_codes", align_bytes=64)
+        w_scales = keep.tile([P, PASSES * O], U8, name="w_scales", align_bytes=64)
+        squares = keep.tile([P, D], BF16, name="squares")
+
+        def g_matmuls(c, j, a, b):
+            cols = proj_raw[c][:].rearrange("p (j a u q e) -> p j a u e q", j=PACK, a=PASSES, u=2, e=2)
+            ps = bank(b)
+            for u in range(2):
+                for e in range(2):
+                    w = 2 * u + e
+                    nc.tensor.matmul(
+                        out=ps[:, w * P : (w + 1) * P],
+                        lhsT=cols[:, j, a, u, e, :],
+                        rhs=diag[:, PACK * c + j, :],
+                        start=True,
+                        stop=True,
+                    )
+            live[("g", c, j, a)] = ps
+
+        def g_out(c, j, a):
+            lo = ((c * PASSES + a) * CHUNK + j * P) * PACK
+            copy_out(
+                g_grouped[:, lo : lo + P * PACK].rearrange("q (p w) -> q p w", w=PACK),
+                live[("g", c, j, a)][:].rearrange("q (w p) -> q p w", w=PACK),
+            )
+
+        def g_quantise(c):
+            lo = c * PASSES * CHUNK
+            width = PASSES * CHUNK
+            count("V", width)
+            nc.vector.quantize_mx(
+                out=g_codes[:, lo : lo + width].bitcast(FP8X4),
+                scales=g_scales[:, lo : lo + width],
+                in_=g_grouped[:, lo * PACK : (lo + width) * PACK],
+            )
+
+        def norm(k, n):
+            acc = const.tile([P, 1], F32, name="norm%d_%d" % (k, n))
+            count("S", D)
+            nc.scalar.activation(
+                out=squares[:], in_=chunk_raw[k][:, n * D : (n + 1) * D], func=ACT.Square, accum_out=acc[:]
+            )
+            live[("norm", k, n)] = acc
+
+        def transposes(k, n, b):
+            words = chunk_raw[k][:].bitcast(F32)
+            ps = bank(b)
+            for v in range(4):
+                lo = (D // 2) * n + P * v
+                nc.tensor.transpose(ps[:, P * v : P * (v + 1)], words[:, lo : lo + P], ident[:])
+            live[("transposed", k, n)] = ps
+
+        def transposes_out(k, n):
+            if n == 0:
+                live[("grouped", k)] = work.tile([P, PASSES * CHUNK * PACK], BF16, name="grouped", align_bytes=64)
+            words = live[("grouped", k)][:].bitcast(F32).rearrange("q (a t u) -> q a t u", a=PASSES, u=2)
+            copy_out(
+                words[:, :, n * P : (n + 1) * P, :],
+                live[("transposed", k, n)][:].rearrange("q (a u t) -> q a t u", a=PASSES, u=2),
+            )
+
+        def quantise_input(k):
+            codes = work.tile([P, PASSES * CHUNK], U32, name="in_codes", align_bytes=64)
+            scales = work.tile([P, PASSES * CHUNK], U8, name="in_scales", align_bytes=64)
+            count("V", PASSES * CHUNK)
+            nc.vector.quantize_mx(out=codes[:].bitcast(FP8X4), scales=scales[:], in_=live[("grouped", k)][:])
+            live[("in", k)] = (codes, scales)
+
+        def spread_norms(k, b):
+            ps = bank(b)
+            for n in range(ROWS):
+                nc.tensor.transpose(
+                    ps[:, n * P : (n + 1) * P], live[("norm", k, n)][:, 0:1].to_broadcast([P, P]), ident[:]
+                )
+            live[("spread", k)] = ps
+
+        def spread_norms_out(k):
+            row = work.tile([P, CHUNK], F32, name="norm_row", bufs=3)
+            copy_out(row[:], live[("spread", k)][:])
+            live[("row", k)] = row
+
+        rounds = [(k, c, 0, CHUNK) for k in range(CHUNKS) for c in range(PASSES)]
+        rounds[-1:] = [(CHUNKS - 1, 1, 0, CHUNK // 2), (CHUNKS - 1, 1, CHUNK // 2, CHUNK // 2)]
+        n_banks1 = PACK * len(rounds)
+        gpsimd_rounds = len(rounds) - 2
+
+        def first_stage(i):
+            rd, j = divmod(i, PACK)
+            k, c, t0, wid = rounds[rd]
+            codes, scales = live[("in", k)]
+            ps = bank(S1_BANKS[i % len(S1_BANKS)])
+            for a in range(PASSES):
+                lo = (c * PASSES + a) * CHUNK + j * P
+                nc.tensor.matmul_mx(
+                    out=ps[:, 0:wid],
+                    lhsT=g_codes[:, lo : lo + P].bitcast(FP8X4),
+                    lhsT_scale=g_scales[:, lo : lo + P],
+                    rhs=codes[:, a * CHUNK + t0 : a * CHUNK + t0 + wid].bitcast(FP8X4),
+                    rhs_scale=scales[:, a * CHUNK + t0 : a * CHUNK + t0 + wid],
+                    start=(a == 0),
+                    stop=(a == PASSES - 1),
+                )
+            live[("dot", i)] = ps
+
+        def correct(i):
+            rd, j = divmod(i, PACK)
+            k, c, t0, wid = rounds[rd]
+            cj = PACK * c + j
+            exponent = work.tile([P, CHUNK], F32, name="exponent", bufs=EXP_LAG + 2)
+            count("V", wid)
+            nc.vector.scalar_tensor_tensor(
+                out=exponent[:, 0:wid],
+                in0=live[("row", k)][:, t0 : t0 + wid],
+                scalar=neg_half_sq[:, cj : cj + 1],
+                in1=live[("dot", i)][:, 0:wid],
+                op0=ALU.mult,
+                op1=ALU.add,
+            )
+            live[("exponent", i)] = exponent
+
+        def exponential(i):
+            rd, j = divmod(i, PACK)
+            k, c, t0, wid = rounds[rd]
+            cj = PACK * c + j
+            count("S", wid)
+            if j == 0:
+                live[("planes", rd)] = work.tile([P, PACK, CHUNK], BF16, name="planes")
+            nc.scalar.activation(
+                out=live[("planes", rd)][:, j, 0:wid],
+                in_=live[("exponent", i)][:, 0:wid],
+                func=ACT.Exp,
+                bias=exp_bias[:, cj : cj + 1],
+                scale=1.0,
+            )
+
+        def interleave(rd):
+            k, c, t0, wid = rounds[rd]
+            side = work.tile([P, CHUNK * PACK], BF16, name="side", bufs=1, align_bytes=64)
+            planes = live[("planes", rd)]
+            if rd < gpsimd_rounds:
+                nc.gpsimd.tensor_scalar(
+                    out=side[:, 0 : wid * PACK].rearrange("p (t j) -> p t j", j=PACK),
+                    in0=planes[:, :, 0:wid].rearrange("p j t -> p t j"),
+                    scalar1=1.0,
+                    scalar2=0.0,
+                    op0=ALU.mult,
+                    op1=ALU.add,
+                )
+            else:
+                count("V", 2 * wid)
+                nc.vector.tensor_copy(
+                    out=side[:, 0 : wid * PACK].rearrange("p (l f j) -> p l j f", f=4, j=PACK),
+                    in_=planes[:, :, 0:wid].rearrange("p j (l f) -> p l j f", f=4),
+                )
+            live[("side", rd)] = side
+
+        def quantise_round(rd):
+            k, c, t0, wid = rounds[rd]
+            count("V", wid)
+            if k < W_CHUNKS:
+                codes, scales, lo = w_codes, w_scales, c * O + k * CHUNK
+            else:
+                if c == 0:
+                    live[("feats", k)] = (
+                        work.tile([P, PASSES * CHUNK], U32, name="f_codes", align_bytes=64),
+                        work.tile([P, PASSES * CHUNK], U8, name="f_scales", align_bytes=64),
+                    )
+                codes, scales = live[("feats", k)]
+                lo = c * CHUNK + t0
+            nc.vector.quantize_mx(
+                out=codes[:, lo : lo + wid].bitcast(FP8X4),
+                scales=scales[:, lo : lo + wid],
+                in_=live[("side", rd)][:, 0 : wid * PACK],
+            )
+
+        n_banks2 = (CHUNKS - W_CHUNKS) * PER_CHUNK
+        last_banks2 = PER_CHUNK // 2
+
+        def second_stage(s, b, passes):
+            m, nh = divmod(s, PER_CHUNK)
+            n, h = divmod(nh, 2)
+            codes, scales = live[("feats", m + W_CHUNKS)]
+            if passes[0] == 0:
+                live[("out", s)] = bank(b)
+            for c in passes:
+                lo = c * CHUNK + n * P
+                wlo = c * O + h * CHUNK
+                nc.tensor.matmul_mx(
+                    out=live[("out", s)][:],
+                    lhsT=codes[:, lo : lo + P].bitcast(FP8X4),
+                    lhsT_scale=scales[:, lo : lo + P],
+                    rhs=w_codes[:, wlo : wlo + CHUNK].bitcast(FP8X4),
+                    rhs_scale=w_scales[:, wlo : wlo + CHUNK],
+                    start=(c == 0),
+                    stop=(c == PASSES - 1),
+                )
+
+        def second_stage_out(s):
+            m, nh = divmod(s, PER_CHUNK)
+            n, h = divmod(nh, 2)
+            if h == 0:
+                live[("staged", m, n)] = work.tile([P, O], F32, name="staged", bufs=8)
+            staged = live[("staged", m, n)]
+            half = slice(h * CHUNK, (h + 1) * CHUNK)
+            copy_out(staged[:, half], live[("out", s)][:])
+            dst = out_rows[m * CHUNK : (m + 1) * CHUNK, :].rearrange("(p n) o -> p n o", n=ROWS)
+            if s >= n_banks2 - last_banks2:
+                nc.sync.dma_start(out=dst[:, n, half], in_=staged[:, half])
+            elif h == 1:
+                nc.sync.dma_start(out=dst[:, n, :], in_=staged[:])
+
+        for ja in range(PER_CHUNK):
+            g_matmuls(0, ja // PASSES, ja % PASSES, ja)
+        for ja in range(PER_CHUNK):
+            g_out(0, ja // PASSES, ja % PASSES)
+        g_quantise(0)
+        for n in range(ROWS):
+            transposes(0, n, n)
+        for n in range(ROWS):
+            norm(0, n)
+            transposes_out(0, n)
+        quantise_input(0)
+        for ja in range(PER_CHUNK):
+            g_matmuls(1, ja // PASSES, ja % PASSES, (ROWS + ja) % BANKS)
+        for ja in range(PER_CHUNK):
+            g_out(1, ja // PASSES, ja % PASSES)
+        g_quantise(1)
+        spread_norms(0, S2_BANKS[1])
+        spread_norms_out(0)
+        in_head = (0, 1)
+        for n in in_head:
+            transposes(1, n, T_BANKS[n])
+        for n in in_head:
+            transposes_out(1, n)
+        for n in in_head:
+            norm(1, n)
+
+        norm_ticks = {-3: 0, -1: 1, 1: 2, 3: 3}
+        for i in range(-LEAD, S2_FIRST + n_banks2 - last_banks2):
+            k, step = divmod(i, PER_CHUNK)
+            nxt = k + 1 if i >= 0 and k + 1 < CHUNKS else None
+            s = i - S2_FIRST
+            if s >= 0:
+                second_stage(s, S2_BANKS[s % len(S2_BANKS)], (0, 1))
+            if i + LEAD < n_banks1:
+                first_stage(i + LEAD)
+            if i >= 0 and step == 6 and k + 2 < CHUNKS:
+                transposes(k + 2, 0, T_BANKS[0])
+                transposes(k + 2, 1, T_BANKS[1])
+            if nxt and step == 1:
+                transposes(nxt, 2, T_BANKS[0])
+                transposes(nxt, 3, T_BANKS[1])
+            if nxt and step == 4:
+                spread_norms(nxt, T_BANKS[0])
+            if 0 <= i < n_banks1:
+                correct(i)
+            if 0 <= i - EXP_LAG < n_banks1:
+                exponential(i - EXP_LAG)
+            rd, rest = divmod(i - EXP_LAG - (PACK - 1), PACK)
+            if rest == 0 and 0 <= rd < gpsimd_rounds:
+                interleave(rd)
+            rd, rest = divmod(i - EXP_LAG - (PACK - 1) - QUANT_LAG, PACK)
+            if rest == 0 and 0 <= rd < gpsimd_rounds:
+                quantise_round(rd)
+            rd, rest = divmod(i - EXP_LAG - (PACK - 1) - 1, PACK)
+            if rest == 0 and gpsimd_rounds <= rd < len(rounds):
+                interleave(rd)
+            rd, rest = divmod(i - EXP_LAG - (PACK - 1) - 2, PACK)
+            if rest == 0 and gpsimd_rounds <= rd < len(rounds):
+                quantise_round(rd)
+            if nxt and step == 4:
+                quantise_input(nxt)
+            if i >= 0 and step == 7 and k + 2 < CHUNKS:
+                transposes_out(k + 2, 0)
+            if i >= PER_CHUNK and step == 0 and nxt:
+                transposes_out(nxt, 1)
+            if nxt and step == 2:
+                transposes_out(nxt, 2)
+            if nxt and step == 3:
+                transposes_out(nxt, 3)
+            if nxt and step == 5:
+                spread_norms_out(nxt)
+            if s >= 1:
+                second_stage_out(s - 1)
+            for later in range(1, CHUNKS):
+                n = norm_ticks.get(i - PER_CHUNK * (later - 1))
+                if n is not None and not (later == 1 and n in in_head):
+                    norm(later, n)
+
+        second_stage_out(n_banks2 - last_banks2 - 1)
+        end_banks = T_BANKS + S1_BANKS[:2]
+        last = range(n_banks2 - last_banks2, n_banks2)
+        for s in last:
+            second_stage(s, end_banks[s - last[0]], (0,))
+        for s in last:
+            second_stage(s, end_banks[s - last[0]], (1,))
+        for s in last:
+            second_stage_out(s)

@@ -27,6 +27,23 @@ PER_CHUNK = PASSES * PACK
 
 FLOPS = 2 * (O * D * R + T * D * R + T * R * O)
 
+G1_BANKS = (7, 5, 3, 4)
+ORDER = (0, 1, 2, 3, 4, 5)
+LAST_WIDTHS = (256, 128, 128)
+END_RATE = 2
+HOLD = 1
+HOLD_TICK = 38
+HOLD_END = 2
+FREE_TICK = 38
+EARLY_TICK = 52
+FRONT = {
+    "turn": {-9: (0, 1), -7: (2, 3)},
+    "turn_out": {-8: (0,), -7: (1,), -6: (2,), -5: (3,)},
+    "quantise": {-4: (0,)},
+    "spread": {-4: (0,)},
+    "spread_out": {-3: (0,)},
+    "norm": {-11: (0,), -9: (1,), -7: (2,), -5: (3,)},
+}
 BANKS = 8
 S1_BANKS = (0, 1, 2)
 S2_BANKS = (3, 4, 5)
@@ -36,7 +53,7 @@ WARM_UP = 4
 LEAD = 2
 EXP_LAG = 2
 QUANT_LAG = 3
-S2_FIRST = 3 * PER_CHUNK + EXP_LAG + QUANT_LAG
+S2_XX = 3 * PER_CHUNK + EXP_LAG + QUANT_LAG
 
 
 def tile_nnk_kernel(tc, x, input_weights, xis, proj_matrix, out):
@@ -65,8 +82,8 @@ def tile_nnk_kernel(tc, x, input_weights, xis, proj_matrix, out):
         def idler():
             return "V" if queued["V"] <= queued["S"] else "S"
 
-        def copy_out(dst, src):
-            eng = idler()
+        def copy_out(dst, src, eng=None):
+            eng = eng or idler()
             count(eng, CHUNK)
             if eng == "V":
                 nc.vector.tensor_copy(out=dst, in_=src)
@@ -78,30 +95,31 @@ def tile_nnk_kernel(tc, x, input_weights, xis, proj_matrix, out):
         proj_raw = []
         chunk_raw = []
 
-        def load_proj(c, pieces):
-            raw = raws.tile([P, PACK * D], BF16, name="proj_raw%d" % c)
-            src = proj_matrix[c * CHUNK : (c + 1) * CHUNK, :].rearrange("(p j) d -> p j d", j=PACK)
-            dst = raw[:].rearrange("p (j d) -> p j d", j=PACK)
-            rows = PACK // pieces
-            for j in range(0, PACK, rows):
-                nc.sync.dma_start(out=dst[:, j : j + rows, :], in_=src[:, j : j + rows, :])
-            proj_raw.append(raw)
+        for c in range(PASSES):
+            proj_raw.append(raws.tile([P, PACK * D], BF16, name="proj_raw%d" % c))
+        for k in range(CHUNKS):
+            chunk_raw.append(raws.tile([P, ROWS * D], BF16, name="chunk_raw%d" % k))
 
-        def load_chunk(k):
-            raw = raws.tile([P, ROWS * D], BF16, name="chunk_raw%d" % k)
+        def load_proj(c, j, rows):
+            src = proj_matrix[c * CHUNK : (c + 1) * CHUNK, :].rearrange("(p j) d -> p j d", j=PACK)
+            dst = proj_raw[c][:].rearrange("p (j d) -> p j d", j=PACK)
+            nc.sync.dma_start(out=dst[:, j : j + rows, :], in_=src[:, j : j + rows, :])
+
+        def load_chunk(k, n, groups):
             if k < W_CHUNKS:
                 src = input_weights[k * CHUNK : (k + 1) * CHUNK, :].rearrange("(n p) d -> p n d", p=P)
             else:
                 m = k - W_CHUNKS
                 src = x_rows[m * CHUNK : (m + 1) * CHUNK, :].rearrange("(p n) d -> p n d", n=ROWS)
-            nc.sync.dma_start(out=raw[:].rearrange("p (n d) -> p n d", n=ROWS), in_=src)
-            chunk_raw.append(raw)
+            dst = chunk_raw[k][:].rearrange("p (n d) -> p n d", n=ROWS)
+            nc.sync.dma_start(out=dst[:, n : n + groups, :], in_=src[:, n : n + groups, :])
 
-        load_proj(0, PACK)
-        load_chunk(0)
-        load_proj(1, 1)
+        for n in range(ROWS):
+            load_proj(0, n, 1)
+            load_chunk(0, n, 1)
+        load_proj(1, 0, PACK)
         for k in range(1, CHUNKS):
-            load_chunk(k)
+            load_chunk(k, 0, ROWS)
 
         ident = const.tile([P, P], F32, name="ident")
         make_identity(nc, ident[:])
@@ -115,9 +133,6 @@ def tile_nnk_kernel(tc, x, input_weights, xis, proj_matrix, out):
             nc.tensor.matmul(out=idle[:], lhsT=zeros[:, 0:P], rhs=zeros[:], start=True, stop=True)
         xis32 = const.tile([P, PER_CHUNK], F32, name="xis32")
         nc.vector.tensor_copy(out=xis32[:], in_=xis_bf[:].rearrange("p c j -> p (c j)"))
-        diag = const.tile([P, PER_CHUNK, P], BF16, name="diag")
-        for cj in range(PER_CHUNK):
-            nc.vector.tensor_scalar_mul(out=diag[:, cj, :], in0=ident[:], scalar1=xis32[:, cj : cj + 1])
         neg_half_sq = const.tile([P, PER_CHUNK], F32, name="neg_half_sq")
         nc.vector.scalar_tensor_tensor(
             out=neg_half_sq[:], in0=xis32[:], scalar=-0.5, in1=xis32[:], op0=ALU.mult, op1=ALU.mult
@@ -132,26 +147,31 @@ def tile_nnk_kernel(tc, x, input_weights, xis, proj_matrix, out):
         w_scales = keep.tile([P, PASSES * O], U8, name="w_scales", align_bytes=64)
         squares = keep.tile([P, D], BF16, name="squares")
 
-        def g_matmuls(c, j, a, b):
-            cols = proj_raw[c][:].rearrange("p (j a u q e) -> p j a u e q", j=PACK, a=PASSES, u=2, e=2)
+        def word_transposes(rows, n, b):
+            words = rows[:].bitcast(F32)
             ps = bank(b)
-            for u in range(2):
-                for e in range(2):
-                    w = 2 * u + e
-                    nc.tensor.matmul(
-                        out=ps[:, w * P : (w + 1) * P],
-                        lhsT=cols[:, j, a, u, e, :],
-                        rhs=diag[:, PACK * c + j, :],
-                        start=True,
-                        stop=True,
-                    )
-            live[("g", c, j, a)] = ps
+            for v in range(4):
+                lo = (D // 2) * n + P * v
+                nc.tensor.transpose(ps[:, P * v : P * (v + 1)], words[:, lo : lo + P], ident[:])
+            return ps
 
-        def g_out(c, j, a):
-            lo = ((c * PASSES + a) * CHUNK + j * P) * PACK
+        g_rows = [raws.tile([P, PACK * D], BF16, name="g_rows%d" % c) for c in range(PASSES)]
+
+        def g_scale(c, j):
+            cols = slice(j * D, (j + 1) * D)
+            cj = PACK * c + j
+            count("V", D // 4)
+            nc.vector.tensor_scalar_mul(out=g_rows[c][:, cols], in0=proj_raw[c][:, cols], scalar1=xis32[:, cj : cj + 1])
+
+        def g_transposes(c, j, b):
+            live[("g", c, j)] = word_transposes(g_rows[c], j, b)
+
+        def g_out(c, j, eng=None):
+            words = g_grouped[:].bitcast(F32).rearrange("q (b t u) -> q b t u", b=PASSES * PASSES, u=2)
             copy_out(
-                g_grouped[:, lo : lo + P * PACK].rearrange("q (p w) -> q p w", w=PACK),
-                live[("g", c, j, a)][:].rearrange("q (w p) -> q p w", w=PACK),
+                words[:, c * PASSES : (c + 1) * PASSES, j * P : (j + 1) * P, :],
+                live[("g", c, j)][:].rearrange("q (a u t) -> q a t u", a=PASSES, u=2),
+                eng,
             )
 
         def g_quantise(c):
@@ -173,12 +193,7 @@ def tile_nnk_kernel(tc, x, input_weights, xis, proj_matrix, out):
             live[("norm", k, n)] = acc
 
         def transposes(k, n, b):
-            words = chunk_raw[k][:].bitcast(F32)
-            ps = bank(b)
-            for v in range(4):
-                lo = (D // 2) * n + P * v
-                nc.tensor.transpose(ps[:, P * v : P * (v + 1)], words[:, lo : lo + P], ident[:])
-            live[("transposed", k, n)] = ps
+            live[("transposed", k, n)] = word_transposes(chunk_raw[k], n, b)
 
         def transposes_out(k, n):
             if n == 0:
@@ -204,15 +219,19 @@ def tile_nnk_kernel(tc, x, input_weights, xis, proj_matrix, out):
                 )
             live[("spread", k)] = ps
 
-        def spread_norms_out(k):
+        def spread_norms_out(k, eng=None):
             row = work.tile([P, CHUNK], F32, name="norm_row", bufs=3)
-            copy_out(row[:], live[("spread", k)][:])
+            copy_out(row[:], live[("spread", k)][:], eng)
             live[("row", k)] = row
 
-        rounds = [(k, c, 0, CHUNK) for k in range(CHUNKS) for c in range(PASSES)]
-        rounds[-1:] = [(CHUNKS - 1, 1, 0, CHUNK // 2), (CHUNKS - 1, 1, CHUNK // 2, CHUNK // 2)]
+        rounds = [(k, c, 0, CHUNK) for k in ORDER for c in range(PASSES)]
+        rounds.pop()
+        first_token = 0
+        for width in LAST_WIDTHS:
+            rounds.append((ORDER[-1], 1, first_token, width))
+            first_token += width
         n_banks1 = PACK * len(rounds)
-        gpsimd_rounds = len(rounds) - 2
+        gpsimd_rounds = len(rounds) - len(LAST_WIDTHS)
 
         def first_stage(i):
             rd, j = divmod(i, PACK)
@@ -303,20 +322,16 @@ def tile_nnk_kernel(tc, x, input_weights, xis, proj_matrix, out):
                 in_=live[("side", rd)][:, 0 : wid * PACK],
             )
 
-        n_banks2 = (CHUNKS - W_CHUNKS) * PER_CHUNK
-        last_banks2 = PER_CHUNK // 2
-
-        def second_stage(s, b, passes):
-            m, nh = divmod(s, PER_CHUNK)
-            n, h = divmod(nh, 2)
+        def second_stage(item, b, passes):
+            m, n, h = item
             codes, scales = live[("feats", m + W_CHUNKS)]
             if passes[0] == 0:
-                live[("out", s)] = bank(b)
+                live[("out", item)] = bank(b)
             for c in passes:
                 lo = c * CHUNK + n * P
                 wlo = c * O + h * CHUNK
                 nc.tensor.matmul_mx(
-                    out=live[("out", s)][:],
+                    out=live[("out", item)][:],
                     lhsT=codes[:, lo : lo + P].bitcast(FP8X4),
                     lhsT_scale=scales[:, lo : lo + P],
                     rhs=w_codes[:, wlo : wlo + CHUNK].bitcast(FP8X4),
@@ -325,104 +340,137 @@ def tile_nnk_kernel(tc, x, input_weights, xis, proj_matrix, out):
                     stop=(c == PASSES - 1),
                 )
 
-        def second_stage_out(s):
-            m, nh = divmod(s, PER_CHUNK)
-            n, h = divmod(nh, 2)
-            if h == 0:
-                live[("staged", m, n)] = work.tile([P, O], F32, name="staged", bufs=8)
-            staged = live[("staged", m, n)]
-            half = slice(h * CHUNK, (h + 1) * CHUNK)
-            copy_out(staged[:, half], live[("out", s)][:])
+        def second_stage_out(item):
+            m, n, h = item
+            staged = work.tile([P, CHUNK], F32, name="staged", bufs=12)
+            copy_out(staged[:], live[("out", item)][:])
             dst = out_rows[m * CHUNK : (m + 1) * CHUNK, :].rearrange("(p n) o -> p n o", n=ROWS)
-            if s >= n_banks2 - last_banks2:
-                nc.sync.dma_start(out=dst[:, n, half], in_=staged[:, half])
-            elif h == 1:
-                nc.sync.dma_start(out=dst[:, n, :], in_=staged[:])
+            nc.sync.dma_start(out=dst[:, n, h * CHUNK : (h + 1) * CHUNK], in_=staged[:])
 
-        for ja in range(PER_CHUNK):
-            g_matmuls(0, ja // PASSES, ja % PASSES, ja)
-        for ja in range(PER_CHUNK):
-            g_out(0, ja // PASSES, ja % PASSES)
+        for n in range(ROWS + 1):
+            if n < ROWS:
+                g_scale(0, n)
+                g_transposes(0, n, n)
+                transposes(0, n, ROWS + n)
+                norm(0, n)
+            if n > 0:
+                g_out(0, n - 1)
+                transposes_out(0, n - 1)
+        spread_norms(0, ROWS)
+        spread_norms_out(0, "S")
+        def g1(j):
+            g_scale(1, j)
+            g_transposes(1, j, G1_BANKS[j])
+
+        g1(0)
+        g1(1)
         g_quantise(0)
-        for n in range(ROWS):
-            transposes(0, n, n)
-        for n in range(ROWS):
-            norm(0, n)
-            transposes_out(0, n)
+        g1(2)
+        g1(3)
         quantise_input(0)
-        for ja in range(PER_CHUNK):
-            g_matmuls(1, ja // PASSES, ja % PASSES, (ROWS + ja) % BANKS)
-        for ja in range(PER_CHUNK):
-            g_out(1, ja // PASSES, ja % PASSES)
-        g_quantise(1)
-        spread_norms(0, S2_BANKS[1])
-        spread_norms_out(0)
-        in_head = (0, 1)
-        for n in in_head:
-            transposes(1, n, T_BANKS[n])
-        for n in in_head:
-            transposes_out(1, n)
-        for n in in_head:
-            norm(1, n)
+        transposes(1, 0, T_BANKS[0])
+        g_out(1, 0, "S")
+        g_out(1, 1, "S")
+        norm(1, 0)
+        g_out(1, 2, "S")
+        g_out(1, 3, "S")
+        transposes_out(1, 0)
 
-        norm_ticks = {-3: 0, -1: 1, 1: 2, 3: 3}
-        for i in range(-LEAD, S2_FIRST + n_banks2 - last_banks2):
-            k, step = divmod(i, PER_CHUNK)
-            nxt = k + 1 if i >= 0 and k + 1 < CHUNKS else None
-            s = i - S2_FIRST
-            if s >= 0:
-                second_stage(s, S2_BANKS[s % len(S2_BANKS)], (0, 1))
+        def due(what, i):
+            found = []
+            for q in range(1, CHUNKS):
+                for offset, groups in FRONT[what].items():
+                    if max(PER_CHUNK * q + offset, -1) == i:
+                        found.extend((ORDER[q], n) for n in groups)
+            return found
+
+        ready_w = []
+        ready_x = []
+        pending = []
+        opened = []
+        s2_free = list(S2_BANKS)
+
+        def release(rd):
+            k, c, t0, wid = rounds[rd]
+            if c == PASSES - 1:
+                if k < W_CHUNKS:
+                    ready_w.append(k)
+                    pending.extend((m, n, k) for m, n in ready_x)
+                else:
+                    groups = [(k - W_CHUNKS, n) for n in range(t0 // P, (t0 + wid) // P)]
+                    ready_x.extend(groups)
+                    pending.extend((m, n, h) for m, n in groups for h in ready_w)
+
+        early = [(ORDER[-1] - W_CHUNKS, ROWS - 1, h) for h in range(W_CHUNKS)]
+        n_items = (CHUNKS - W_CHUNKS) * PER_CHUNK
+        items_out = 0
+        early_banks = []
+        i = -LEAD - 1
+        while items_out < n_items:
+            i += 1
+            assert i < 100
+            new = []
+            rate = 1 if i + LEAD < n_banks1 else END_RATE
+            while pending and s2_free and len(new) < rate:
+                item = pending.pop(0)
+                if item in early:
+                    b = early_banks.pop(0)
+                    second_stage(item, b, (1,))
+                else:
+                    b = s2_free.pop(0)
+                    second_stage(item, b, (0, 1))
+                new.append(item)
+                opened.append((item, b))
+            if i == EARLY_TICK:
+                for item in early:
+                    early_banks.append(s2_free.pop(0))
+                    second_stage(item, early_banks[-1], (0,))
             if i + LEAD < n_banks1:
                 first_stage(i + LEAD)
-            if i >= 0 and step == 6 and k + 2 < CHUNKS:
-                transposes(k + 2, 0, T_BANKS[0])
-                transposes(k + 2, 1, T_BANKS[1])
-            if nxt and step == 1:
-                transposes(nxt, 2, T_BANKS[0])
-                transposes(nxt, 3, T_BANKS[1])
-            if nxt and step == 4:
-                spread_norms(nxt, T_BANKS[0])
+            for k, n in due("turn", i):
+                if (k, n) != (ORDER[1], 0):
+                    transposes(k, n, T_BANKS[n % 2])
+            for k, n in due("spread", i):
+                spread_norms(k, T_BANKS[0])
             if 0 <= i < n_banks1:
                 correct(i)
+            if i == 1:
+                g_quantise(1)
             if 0 <= i - EXP_LAG < n_banks1:
                 exponential(i - EXP_LAG)
             rd, rest = divmod(i - EXP_LAG - (PACK - 1), PACK)
             if rest == 0 and 0 <= rd < gpsimd_rounds:
                 interleave(rd)
-            rd, rest = divmod(i - EXP_LAG - (PACK - 1) - QUANT_LAG, PACK)
-            if rest == 0 and 0 <= rd < gpsimd_rounds:
-                quantise_round(rd)
             rd, rest = divmod(i - EXP_LAG - (PACK - 1) - 1, PACK)
             if rest == 0 and gpsimd_rounds <= rd < len(rounds):
                 interleave(rd)
             rd, rest = divmod(i - EXP_LAG - (PACK - 1) - 2, PACK)
             if rest == 0 and gpsimd_rounds <= rd < len(rounds):
                 quantise_round(rd)
-            if nxt and step == 4:
-                quantise_input(nxt)
-            if i >= 0 and step == 7 and k + 2 < CHUNKS:
-                transposes_out(k + 2, 0)
-            if i >= PER_CHUNK and step == 0 and nxt:
-                transposes_out(nxt, 1)
-            if nxt and step == 2:
-                transposes_out(nxt, 2)
-            if nxt and step == 3:
-                transposes_out(nxt, 3)
-            if nxt and step == 5:
-                spread_norms_out(nxt)
-            if s >= 1:
-                second_stage_out(s - 1)
-            for later in range(1, CHUNKS):
-                n = norm_ticks.get(i - PER_CHUNK * (later - 1))
-                if n is not None and not (later == 1 and n in in_head):
-                    norm(later, n)
-
-        second_stage_out(n_banks2 - last_banks2 - 1)
-        end_banks = T_BANKS + S1_BANKS[:2]
-        last = range(n_banks2 - last_banks2, n_banks2)
-        for s in last:
-            second_stage(s, end_banks[s - last[0]], (0,))
-        for s in last:
-            second_stage(s, end_banks[s - last[0]], (1,))
-        for s in last:
-            second_stage_out(s)
+                release(rd)
+            for k, n in due("turn_out", i):
+                if (k, n) != (ORDER[1], 0):
+                    transposes_out(k, n)
+            for k, n in due("spread_out", i):
+                spread_norms_out(k)
+            hold = HOLD if i < HOLD_TICK else HOLD_END
+            while opened and opened[0][0] not in new and (len(opened) > hold or not new or not s2_free):
+                item, b = opened.pop(0)
+                second_stage_out(item)
+                s2_free.append(b)
+                items_out += 1
+                if len(opened) <= hold:
+                    break
+            if i == FREE_TICK:
+                s2_free.extend(T_BANKS)
+            if i == n_banks1:
+                s2_free.extend(S1_BANKS)
+            rd, rest = divmod(i - EXP_LAG - (PACK - 1) - QUANT_LAG, PACK)
+            if rest == 0 and 0 <= rd < gpsimd_rounds:
+                quantise_round(rd)
+                release(rd)
+            for k, n in due("quantise", i):
+                quantise_input(k)
+            for k, n in due("norm", i):
+                if (k, n) != (ORDER[1], 0):
+                    norm(k, n)

@@ -28,14 +28,6 @@ PER_CHUNK = PASSES * PACK
 FLOPS = 2 * (O * D * R + T * D * R + T * R * O)
 
 G1_BANKS = (7, 5, 3, 4)
-ORDER = (0, 1, 2, 3, 4, 5)
-LAST_WIDTHS = (256, 128, 128)
-END_RATE = 2
-HOLD = 1
-HOLD_TICK = 38
-HOLD_END = 2
-FREE_TICK = 38
-EARLY_TICK = 52
 FRONT = {
     "turn": {-9: (0, 1), -7: (2, 3)},
     "turn_out": {-8: (0,), -7: (1,), -6: (2,), -5: (3,)},
@@ -53,7 +45,7 @@ WARM_UP = 4
 LEAD = 2
 EXP_LAG = 2
 QUANT_LAG = 3
-S2_XX = 3 * PER_CHUNK + EXP_LAG + QUANT_LAG
+S2_FIRST = 3 * PER_CHUNK + EXP_LAG + QUANT_LAG
 
 
 def tile_nnk_kernel(tc, x, input_weights, xis, proj_matrix, out):
@@ -224,14 +216,10 @@ def tile_nnk_kernel(tc, x, input_weights, xis, proj_matrix, out):
             copy_out(row[:], live[("spread", k)][:], eng)
             live[("row", k)] = row
 
-        rounds = [(k, c, 0, CHUNK) for k in ORDER for c in range(PASSES)]
-        rounds.pop()
-        first_token = 0
-        for width in LAST_WIDTHS:
-            rounds.append((ORDER[-1], 1, first_token, width))
-            first_token += width
+        rounds = [(k, c, 0, CHUNK) for k in range(CHUNKS) for c in range(PASSES)]
+        rounds[-1:] = [(CHUNKS - 1, 1, 0, CHUNK // 2), (CHUNKS - 1, 1, CHUNK // 2, CHUNK // 2)]
         n_banks1 = PACK * len(rounds)
-        gpsimd_rounds = len(rounds) - len(LAST_WIDTHS)
+        gpsimd_rounds = len(rounds) - 2
 
         def first_stage(i):
             rd, j = divmod(i, PACK)
@@ -322,16 +310,20 @@ def tile_nnk_kernel(tc, x, input_weights, xis, proj_matrix, out):
                 in_=live[("side", rd)][:, 0 : wid * PACK],
             )
 
-        def second_stage(item, b, passes):
-            m, n, h = item
+        n_banks2 = (CHUNKS - W_CHUNKS) * PER_CHUNK
+        last_banks2 = PER_CHUNK // 2
+
+        def second_stage(s, b, passes):
+            m, nh = divmod(s, PER_CHUNK)
+            n, h = divmod(nh, 2)
             codes, scales = live[("feats", m + W_CHUNKS)]
             if passes[0] == 0:
-                live[("out", item)] = bank(b)
+                live[("out", s)] = bank(b)
             for c in passes:
                 lo = c * CHUNK + n * P
                 wlo = c * O + h * CHUNK
                 nc.tensor.matmul_mx(
-                    out=live[("out", item)][:],
+                    out=live[("out", s)][:],
                     lhsT=codes[:, lo : lo + P].bitcast(FP8X4),
                     lhsT_scale=scales[:, lo : lo + P],
                     rhs=w_codes[:, wlo : wlo + CHUNK].bitcast(FP8X4),
@@ -340,12 +332,19 @@ def tile_nnk_kernel(tc, x, input_weights, xis, proj_matrix, out):
                     stop=(c == PASSES - 1),
                 )
 
-        def second_stage_out(item):
-            m, n, h = item
-            staged = work.tile([P, CHUNK], F32, name="staged", bufs=12)
-            copy_out(staged[:], live[("out", item)][:])
+        def second_stage_out(s):
+            m, nh = divmod(s, PER_CHUNK)
+            n, h = divmod(nh, 2)
+            if h == 0:
+                live[("staged", m, n)] = work.tile([P, O], F32, name="staged", bufs=8)
+            staged = live[("staged", m, n)]
+            half = slice(h * CHUNK, (h + 1) * CHUNK)
+            copy_out(staged[:, half], live[("out", s)][:])
             dst = out_rows[m * CHUNK : (m + 1) * CHUNK, :].rearrange("(p n) o -> p n o", n=ROWS)
-            nc.sync.dma_start(out=dst[:, n, h * CHUNK : (h + 1) * CHUNK], in_=staged[:])
+            if s >= n_banks2 - last_banks2:
+                nc.sync.dma_start(out=dst[:, n, half], in_=staged[:, half])
+            elif h == 1:
+                nc.sync.dma_start(out=dst[:, n, :], in_=staged[:])
 
         for n in range(ROWS + 1):
             if n < ROWS:
@@ -378,57 +377,20 @@ def tile_nnk_kernel(tc, x, input_weights, xis, proj_matrix, out):
 
         def due(what, i):
             found = []
-            for q in range(1, CHUNKS):
+            for k in range(1, CHUNKS):
                 for offset, groups in FRONT[what].items():
-                    if max(PER_CHUNK * q + offset, -1) == i:
-                        found.extend((ORDER[q], n) for n in groups)
+                    if max(PER_CHUNK * k + offset, -1) == i:
+                        found.extend((k, n) for n in groups)
             return found
 
-        ready_w = []
-        ready_x = []
-        pending = []
-        opened = []
-        s2_free = list(S2_BANKS)
-
-        def release(rd):
-            k, c, t0, wid = rounds[rd]
-            if c == PASSES - 1:
-                if k < W_CHUNKS:
-                    ready_w.append(k)
-                    pending.extend((m, n, k) for m, n in ready_x)
-                else:
-                    groups = [(k - W_CHUNKS, n) for n in range(t0 // P, (t0 + wid) // P)]
-                    ready_x.extend(groups)
-                    pending.extend((m, n, h) for m, n in groups for h in ready_w)
-
-        early = [(ORDER[-1] - W_CHUNKS, ROWS - 1, h) for h in range(W_CHUNKS)]
-        n_items = (CHUNKS - W_CHUNKS) * PER_CHUNK
-        items_out = 0
-        early_banks = []
-        i = -LEAD - 1
-        while items_out < n_items:
-            i += 1
-            assert i < 100
-            new = []
-            rate = 1 if i + LEAD < n_banks1 else END_RATE
-            while pending and s2_free and len(new) < rate:
-                item = pending.pop(0)
-                if item in early:
-                    b = early_banks.pop(0)
-                    second_stage(item, b, (1,))
-                else:
-                    b = s2_free.pop(0)
-                    second_stage(item, b, (0, 1))
-                new.append(item)
-                opened.append((item, b))
-            if i == EARLY_TICK:
-                for item in early:
-                    early_banks.append(s2_free.pop(0))
-                    second_stage(item, early_banks[-1], (0,))
+        for i in range(-LEAD, S2_FIRST + n_banks2 - last_banks2):
+            s = i - S2_FIRST
+            if s >= 0:
+                second_stage(s, S2_BANKS[s % len(S2_BANKS)], (0, 1))
             if i + LEAD < n_banks1:
                 first_stage(i + LEAD)
             for k, n in due("turn", i):
-                if (k, n) != (ORDER[1], 0):
+                if (k, n) != (1, 0):
                     transposes(k, n, T_BANKS[n % 2])
             for k, n in due("spread", i):
                 spread_norms(k, T_BANKS[0])
@@ -447,30 +409,28 @@ def tile_nnk_kernel(tc, x, input_weights, xis, proj_matrix, out):
             rd, rest = divmod(i - EXP_LAG - (PACK - 1) - 2, PACK)
             if rest == 0 and gpsimd_rounds <= rd < len(rounds):
                 quantise_round(rd)
-                release(rd)
-            for k, n in due("turn_out", i):
-                if (k, n) != (ORDER[1], 0):
-                    transposes_out(k, n)
-            for k, n in due("spread_out", i):
-                spread_norms_out(k)
-            hold = HOLD if i < HOLD_TICK else HOLD_END
-            while opened and opened[0][0] not in new and (len(opened) > hold or not new or not s2_free):
-                item, b = opened.pop(0)
-                second_stage_out(item)
-                s2_free.append(b)
-                items_out += 1
-                if len(opened) <= hold:
-                    break
-            if i == FREE_TICK:
-                s2_free.extend(T_BANKS)
-            if i == n_banks1:
-                s2_free.extend(S1_BANKS)
             rd, rest = divmod(i - EXP_LAG - (PACK - 1) - QUANT_LAG, PACK)
             if rest == 0 and 0 <= rd < gpsimd_rounds:
                 quantise_round(rd)
-                release(rd)
             for k, n in due("quantise", i):
                 quantise_input(k)
+            for k, n in due("turn_out", i):
+                if (k, n) != (1, 0):
+                    transposes_out(k, n)
+            for k, n in due("spread_out", i):
+                spread_norms_out(k)
+            if s >= 1:
+                second_stage_out(s - 1)
             for k, n in due("norm", i):
-                if (k, n) != (ORDER[1], 0):
+                if (k, n) != (1, 0):
                     norm(k, n)
+
+        second_stage_out(n_banks2 - last_banks2 - 1)
+        end_banks = T_BANKS + S1_BANKS[:2]
+        last = range(n_banks2 - last_banks2, n_banks2)
+        for s in last:
+            second_stage(s, end_banks[s - last[0]], (0,))
+        for s in last:
+            second_stage(s, end_banks[s - last[0]], (1,))
+        for s in last:
+            second_stage_out(s)

@@ -120,9 +120,12 @@ def tile_nnk_kernel(tc, x, input_weights, xis, proj_matrix, out):
         nc.scalar.activation(out=warm[:], in_=warm[:], func=ACT.Exp)
         zeros = const.tile([P, CHUNK], BF16, name="zeros")
         nc.vector.memset(zeros[:], 0.0)
-        idle = bank(BANKS - 1)
-        for rep in range(WARM_UP):
-            nc.tensor.matmul(out=idle[:], lhsT=zeros[:, 0:P], rhs=zeros[:], start=True, stop=True)
+
+        def keep_warm(b, times):
+            for rep in range(times):
+                nc.tensor.matmul(out=bank(b)[:], lhsT=zeros[:, 0:P], rhs=zeros[:], start=True, stop=True)
+
+        keep_warm(BANKS - 1, WARM_UP)
         xis32 = const.tile([P, PER_CHUNK], F32, name="xis32")
         nc.vector.tensor_copy(out=xis32[:], in_=xis_bf[:].rearrange("p c j -> p (c j)"))
         neg_half_sq = const.tile([P, PER_CHUNK], F32, name="neg_half_sq")
@@ -351,6 +354,7 @@ def tile_nnk_kernel(tc, x, input_weights, xis, proj_matrix, out):
                 g_scale(0, n)
                 g_transposes(0, n, n)
                 transposes(0, n, ROWS + n)
+                keep_warm(BANKS - 1 if n < ROWS - 1 else S1_BANKS[0], 1)
                 norm(0, n)
             if n > 0:
                 g_out(0, n - 1)
@@ -363,11 +367,14 @@ def tile_nnk_kernel(tc, x, input_weights, xis, proj_matrix, out):
 
         g1(0)
         g1(1)
+        keep_warm(S1_BANKS[2], 2)
         g_quantise(0)
         g1(2)
         g1(3)
+        keep_warm(S1_BANKS[2], 1)
         quantise_input(0)
         transposes(1, 0, T_BANKS[0])
+        keep_warm(S1_BANKS[2], 2)
         g_out(1, 0, "S")
         g_out(1, 1, "S")
         norm(1, 0)

@@ -354,7 +354,7 @@ def tile_nnk_kernel(tc, x, input_weights, xis, proj_matrix, out):
                 g_scale(0, n)
                 g_transposes(0, n, n)
                 transposes(0, n, ROWS + n)
-                keep_warm(BANKS - 1 if n < ROWS - 1 else S1_BANKS[0], 1)
+                keep_warm(BANKS - 1 if n < ROWS - 1 else S1_BANKS[0], 2)
                 norm(0, n)
             if n > 0:
                 g_out(0, n - 1)

@@ -22,6 +22,7 @@ CHUNK = 512
 ROWS = CHUNK // P
 PASSES = 2
 W_CHUNKS = O // CHUNK
+SEQ = (("w", 0), ("x", 0), ("w", 1), ("x", 1), ("x", 2), ("x", 3))
 CHUNKS = W_CHUNKS + T // CHUNK
 PER_CHUNK = PASSES * PACK
 
@@ -32,8 +33,8 @@ FRONT = {
     "turn": {-9: (0, 1), -7: (2, 3)},
     "turn_out": {-8: (0,), -7: (1,), -6: (2,), -5: (3,)},
     "quantise": {-4: (0,)},
-    "spread": {-4: (0,)},
-    "spread_out": {-3: (0,)},
+    "spread": {-3: (0,)},
+    "spread_out": {-2: (0,)},
     "norm": {-11: (0,), -9: (1,), -7: (2,), -5: (3,)},
 }
 BANKS = 8
@@ -45,7 +46,6 @@ WARM_UP = 4
 LEAD = 2
 EXP_LAG = 2
 QUANT_LAG = 3
-S2_FIRST = 3 * PER_CHUNK + EXP_LAG + QUANT_LAG
 
 
 def tile_nnk_kernel(tc, x, input_weights, xis, proj_matrix, out):
@@ -98,10 +98,10 @@ def tile_nnk_kernel(tc, x, input_weights, xis, proj_matrix, out):
             nc.sync.dma_start(out=dst[:, j : j + rows, :], in_=src[:, j : j + rows, :])
 
         def load_chunk(k, n, groups):
-            if k < W_CHUNKS:
-                src = input_weights[k * CHUNK : (k + 1) * CHUNK, :].rearrange("(n p) d -> p n d", p=P)
+            kind, m = SEQ[k]
+            if kind == "w":
+                src = input_weights[m * CHUNK : (m + 1) * CHUNK, :].rearrange("(n p) d -> p n d", p=P)
             else:
-                m = k - W_CHUNKS
                 src = x_rows[m * CHUNK : (m + 1) * CHUNK, :].rearrange("(p n) d -> p n d", n=ROWS)
             dst = chunk_raw[k][:].rearrange("p (n d) -> p n d", n=ROWS)
             nc.sync.dma_start(out=dst[:, n : n + groups, :], in_=src[:, n : n + groups, :])
@@ -297,15 +297,16 @@ def tile_nnk_kernel(tc, x, input_weights, xis, proj_matrix, out):
         def quantise_round(rd):
             k, c, t0, wid = rounds[rd]
             count("V", wid)
-            if k < W_CHUNKS:
-                codes, scales, lo = w_codes, w_scales, c * O + k * CHUNK
+            kind, m = SEQ[k]
+            if kind == "w":
+                codes, scales, lo = w_codes, w_scales, c * O + m * CHUNK
             else:
                 if c == 0:
-                    live[("feats", k)] = (
+                    live[("feats", m)] = (
                         work.tile([P, PASSES * CHUNK], U32, name="f_codes", align_bytes=64),
                         work.tile([P, PASSES * CHUNK], U8, name="f_scales", align_bytes=64),
                     )
-                codes, scales = live[("feats", k)]
+                codes, scales = live[("feats", m)]
                 lo = c * CHUNK + t0
             nc.vector.quantize_mx(
                 out=codes[:, lo : lo + wid].bitcast(FP8X4),
@@ -313,13 +314,25 @@ def tile_nnk_kernel(tc, x, input_weights, xis, proj_matrix, out):
                 in_=live[("side", rd)][:, 0 : wid * PACK],
             )
 
-        n_banks2 = (CHUNKS - W_CHUNKS) * PER_CHUNK
+        items = []
+        ticks2 = {}
+
+        def plan(position, found):
+            start = PER_CHUNK * (position + 1) + EXP_LAG + QUANT_LAG
+            for n, item in enumerate(found):
+                ticks2[start + n] = len(items)
+                items.append(item)
+
+        plan(1, [(0, n, 0) for n in range(ROWS)])
+        plan(2, [(0, n, 1) for n in range(ROWS)])
+        for m in range(1, T // CHUNK):
+            plan(m + 2, [(m, n, h) for n in range(ROWS) for h in range(2)])
+        n_banks2 = len(items)
         last_banks2 = PER_CHUNK // 2
 
         def second_stage(s, b, passes):
-            m, nh = divmod(s, PER_CHUNK)
-            n, h = divmod(nh, 2)
-            codes, scales = live[("feats", m + W_CHUNKS)]
+            m, n, h = items[s]
+            codes, scales = live[("feats", m)]
             if passes[0] == 0:
                 live[("out", s)] = bank(b)
             for c in passes:
@@ -336,8 +349,7 @@ def tile_nnk_kernel(tc, x, input_weights, xis, proj_matrix, out):
                 )
 
         def second_stage_out(s):
-            m, nh = divmod(s, PER_CHUNK)
-            n, h = divmod(nh, 2)
+            m, n, h = items[s]
             if h == 0:
                 live[("staged", m, n)] = work.tile([P, O], F32, name="staged", bufs=8)
             staged = live[("staged", m, n)]
@@ -390,12 +402,16 @@ def tile_nnk_kernel(tc, x, input_weights, xis, proj_matrix, out):
                         found.extend((k, n) for n in groups)
             return found
 
-        for i in range(-LEAD, S2_FIRST + n_banks2 - last_banks2):
-            s = i - S2_FIRST
-            if s >= 0:
+        out_next = None
+        for i in range(-LEAD, max(ticks2) + 1 - last_banks2):
+            s = ticks2.get(i)
+            fresh = s is not None and s % PER_CHUNK == 0
+            if s is not None and not fresh:
                 second_stage(s, S2_BANKS[s % len(S2_BANKS)], (0, 1))
             if i + LEAD < n_banks1:
                 first_stage(i + LEAD)
+            if fresh:
+                second_stage(s, S2_BANKS[s % len(S2_BANKS)], (0, 1))
             for k, n in due("turn", i):
                 if (k, n) != (1, 0):
                     transposes(k, n, T_BANKS[n % 2])
@@ -426,8 +442,9 @@ def tile_nnk_kernel(tc, x, input_weights, xis, proj_matrix, out):
                     transposes_out(k, n)
             for k, n in due("spread_out", i):
                 spread_norms_out(k)
-            if s >= 1:
-                second_stage_out(s - 1)
+            if out_next is not None:
+                second_stage_out(out_next)
+            out_next = s
             for k, n in due("norm", i):
                 if (k, n) != (1, 0):
                     norm(k, n)

@@ -42,7 +42,7 @@ S1_BANKS = (0, 1, 2)
 S2_BANKS = (3, 4, 5)
 T_BANKS = (6, 7)
 
-WARM_UP = 4
+WARM_UP = 5
 LEAD = 2
 EXP_LAG = 2
 QUANT_LAG = 3
@@ -383,7 +383,6 @@ def tile_nnk_kernel(tc, x, input_weights, xis, proj_matrix, out):
         g_quantise(0)
         g1(2)
         g1(3)
-        keep_warm(S1_BANKS[2], 1)
         quantise_input(0)
         transposes(1, 0, T_BANKS[0])
         keep_warm(S1_BANKS[2], 2)
@@ -408,6 +407,8 @@ def tile_nnk_kernel(tc, x, input_weights, xis, proj_matrix, out):
             fresh = s is not None and s % PER_CHUNK == 0
             if s is not None and not fresh:
                 second_stage(s, S2_BANKS[s % len(S2_BANKS)], (0, 1))
+            if i < min(ticks2) and due("quantise", i - 2):
+                keep_warm(S2_BANKS[0], 1)
             if i + LEAD < n_banks1:
                 first_stage(i + LEAD)
             if fresh:
@@ -453,8 +454,6 @@ def tile_nnk_kernel(tc, x, input_weights, xis, proj_matrix, out):
         end_banks = T_BANKS + S1_BANKS[:2]
         last = range(n_banks2 - last_banks2, n_banks2)
         for s in last:
-            second_stage(s, end_banks[s - last[0]], (0,))
-        for s in last:
-            second_stage(s, end_banks[s - last[0]], (1,))
+            second_stage(s, end_banks[s - last[0]], (0, 1))
         for s in last:
             second_stage_out(s)

@@ -28,6 +28,7 @@ PER_CHUNK = PASSES * PACK
 
 FLOPS = 2 * (O * D * R + T * D * R + T * R * O)
 
+BANKWISE_STORES = 2
 G1_BANKS = (7, 5, 3, 4)
 FRONT = {
     "turn": {-9: (0, 1), -7: (2, 3)},
@@ -74,9 +75,9 @@ def tile_nnk_kernel(tc, x, input_weights, xis, proj_matrix, out):
         def idler():
             return "V" if queued["V"] <= queued["S"] else "S"
 
-        def copy_out(dst, src, eng=None):
+        def copy_out(dst, src, eng=None, elements=CHUNK):
             eng = eng or idler()
-            count(eng, CHUNK)
+            count(eng, elements)
             if eng == "V":
                 nc.vector.tensor_copy(out=dst, in_=src)
             else:
@@ -323,42 +324,42 @@ def tile_nnk_kernel(tc, x, input_weights, xis, proj_matrix, out):
                 ticks2[start + n] = len(items)
                 items.append(item)
 
-        plan(1, [(0, n, 0) for n in range(ROWS)])
-        plan(2, [(0, n, 1) for n in range(ROWS)])
+        plan(1, [(0, n, 0, CHUNK) for n in range(ROWS)])
+        plan(2, [(0, n, CHUNK, CHUNK) for n in range(ROWS)])
         for m in range(1, T // CHUNK):
-            plan(m + 2, [(m, n, h) for n in range(ROWS) for h in range(2)])
+            plan(m + 2, [(m, n, first, CHUNK) for n in range(ROWS) for first in (0, CHUNK)])
         n_banks2 = len(items)
         last_banks2 = PER_CHUNK // 2
 
-        def second_stage(s, b, passes):
-            m, n, h = items[s]
+        def second_stage(item, b):
+            m, n, first, width = item
             codes, scales = live[("feats", m)]
-            if passes[0] == 0:
-                live[("out", s)] = bank(b)
-            for c in passes:
+            ps = bank(b)
+            for c in range(PASSES):
                 lo = c * CHUNK + n * P
-                wlo = c * O + h * CHUNK
+                wlo = c * O + first
                 nc.tensor.matmul_mx(
-                    out=live[("out", s)][:],
+                    out=ps[:, 0:width],
                     lhsT=codes[:, lo : lo + P].bitcast(FP8X4),
                     lhsT_scale=scales[:, lo : lo + P],
-                    rhs=w_codes[:, wlo : wlo + CHUNK].bitcast(FP8X4),
-                    rhs_scale=w_scales[:, wlo : wlo + CHUNK],
+                    rhs=w_codes[:, wlo : wlo + width].bitcast(FP8X4),
+                    rhs_scale=w_scales[:, wlo : wlo + width],
                     start=(c == 0),
                     stop=(c == PASSES - 1),
                 )
+            live[("out", item)] = ps
 
-        def second_stage_out(s):
-            m, n, h = items[s]
-            if h == 0:
+        def second_stage_out(item):
+            m, n, first, width = item
+            if first == 0:
                 live[("staged", m, n)] = work.tile([P, O], F32, name="staged", bufs=8)
             staged = live[("staged", m, n)]
-            half = slice(h * CHUNK, (h + 1) * CHUNK)
-            copy_out(staged[:, half], live[("out", s)][:])
+            cols = slice(first, first + width)
+            copy_out(staged[:, cols], live[("out", item)][:, 0:width], elements=width)
             dst = out_rows[m * CHUNK : (m + 1) * CHUNK, :].rearrange("(p n) o -> p n o", n=ROWS)
-            if s >= n_banks2 - last_banks2:
-                nc.sync.dma_start(out=dst[:, n, half], in_=staged[:, half])
-            elif h == 1:
+            if m >= BANKWISE_STORES:
+                nc.sync.dma_start(out=dst[:, n, cols], in_=staged[:, cols])
+            elif first + width == O:
                 nc.sync.dma_start(out=dst[:, n, :], in_=staged[:])
 
         for n in range(ROWS + 1):
@@ -406,13 +407,13 @@ def tile_nnk_kernel(tc, x, input_weights, xis, proj_matrix, out):
             s = ticks2.get(i)
             fresh = s is not None and s % PER_CHUNK == 0
             if s is not None and not fresh:
-                second_stage(s, S2_BANKS[s % len(S2_BANKS)], (0, 1))
+                second_stage(items[s], S2_BANKS[s % len(S2_BANKS)])
             if i < min(ticks2) and due("quantise", i - 2):
                 keep_warm(S2_BANKS[0], 1)
             if i + LEAD < n_banks1:
                 first_stage(i + LEAD)
             if fresh:
-                second_stage(s, S2_BANKS[s % len(S2_BANKS)], (0, 1))
+                second_stage(items[s], S2_BANKS[s % len(S2_BANKS)])
             for k, n in due("turn", i):
                 if (k, n) != (1, 0):
                     transposes(k, n, T_BANKS[n % 2])
@@ -444,16 +445,18 @@ def tile_nnk_kernel(tc, x, input_weights, xis, proj_matrix, out):
             for k, n in due("spread_out", i):
                 spread_norms_out(k)
             if out_next is not None:
-                second_stage_out(out_next)
+                second_stage_out(items[out_next])
             out_next = s
             for k, n in due("norm", i):
                 if (k, n) != (1, 0):
                     norm(k, n)
 
-        second_stage_out(n_banks2 - last_banks2 - 1)
-        end_banks = T_BANKS + S1_BANKS[:2]
-        last = range(n_banks2 - last_banks2, n_banks2)
-        for s in last:
-            second_stage(s, end_banks[s - last[0]], (0, 1))
-        for s in last:
-            second_stage_out(s)
+        second_stage_out(items[n_banks2 - last_banks2 - 1])
+        end_items = items[n_banks2 - last_banks2 :]
+        m, n, first, width = end_items.pop()
+        end_items.extend((m, n, first + e * width // 2, width // 2) for e in range(2))
+        end_banks = T_BANKS + S1_BANKS
+        for item, b in zip(end_items, end_banks):
+            second_stage(item, b)
+        for item in end_items:
+            second_stage_out(item)

@@ -114,14 +114,13 @@ def tile_nnk_kernel(tc, x, input_weights, xis, proj_matrix, out):
         for k in range(1, CHUNKS):
             load_chunk(k, 0, ROWS)
 
+        zeros = const.tile([P, CHUNK], BF16, name="zeros")
+        nc.gpsimd.memset(zeros[:].bitcast(F32), 0.0)
         ident = const.tile([P, P], F32, name="ident")
         make_identity(nc, ident[:])
         warm = const.tile([P, 1], F32, name="warm")
         nc.vector.memset(warm[:], 0.0)
         nc.scalar.activation(out=warm[:], in_=warm[:], func=ACT.Exp)
-        zeros = const.tile([P, CHUNK], BF16, name="zeros")
-        nc.vector.memset(zeros[:], 0.0)
-
         def keep_warm(b, times):
             for rep in range(times):
                 nc.tensor.matmul(out=bank(b)[:], lhsT=zeros[:, 0:P], rhs=zeros[:], start=True, stop=True)

@@ -43,7 +43,7 @@ S1_BANKS = (0, 1, 2)
 S2_BANKS = (3, 4, 5)
 T_BANKS = (6, 7)
 
-WARM_UP = 5
+WARM_UP = 4
 LEAD = 2
 EXP_LAG = 2
 QUANT_LAG = 3
@@ -84,7 +84,7 @@ def tile_nnk_kernel(tc, x, input_weights, xis, proj_matrix, out):
                 nc.scalar.copy(out=dst, in_=src)
 
         xis_bf = const.tile([P, PASSES, PACK], BF16, name="xis_bf")
-        nc.sync.dma_start(out=xis_bf[:], in_=xis.rearrange("(c p j) -> p c j", c=PASSES, p=P, j=PACK))
+        nc.scalar.dma_start(out=xis_bf[:], in_=xis.rearrange("(c p j) -> p c j", c=PASSES, p=P, j=PACK))
         proj_raw = []
         chunk_raw = []
 

import math
from contextlib import ExitStack

import concourse.mybir as mybir
from concourse.masks import make_identity

F32 = mybir.dt.float32
BF16 = mybir.dt.bfloat16
U32 = mybir.dt.uint32
U8 = mybir.dt.uint8
FP8X4 = mybir.dt.float8_e4m3fn_x4
ALU = mybir.AluOpType
ACT = mybir.ActivationFunctionType

P = 128
PACK = 4
D = 1024
R = 1024
O = 1024
T = 2048
CHUNK = 512
ROWS = CHUNK // P
PASSES = 2
W_CHUNKS = O // CHUNK
SEQ = (("w", 0), ("x", 0), ("w", 1), ("x", 1), ("x", 2), ("x", 3))
CHUNKS = W_CHUNKS + T // CHUNK
PER_CHUNK = PASSES * PACK

FLOPS = 2 * (O * D * R + T * D * R + T * R * O)

BANKWISE_STORES = 2
G1_BANKS = (7, 5, 3, 4)
FRONT = {
    "turn": {-9: (0, 1), -7: (2, 3)},
    "turn_out": {-8: (0,), -7: (1,), -6: (2,), -5: (3,)},
    "quantise": {-4: (0,)},
    "spread": {-3: (0,)},
    "spread_out": {-2: (0,)},
    "norm": {-11: (0,), -9: (1,), -7: (2,), -5: (3,)},
}
BANKS = 8
S1_BANKS = (0, 1, 2)
S2_BANKS = (3, 4, 5)
T_BANKS = (6, 7)

WARM_UP = 4
LEAD = 2
EXP_LAG = 2
QUANT_LAG = 3


def tile_nnk_kernel(tc, x, input_weights, xis, proj_matrix, out):
    nc = tc.nc
    x_rows = x.flatten_outer_dims()
    out_rows = out.flatten_outer_dims()

    with ExitStack() as ctx:
        ctx.enter_context(tc.manual_schedule())
        const = ctx.enter_context(tc.tile_pool(name="const", bufs=1))
        raws = ctx.enter_context(tc.tile_pool(name="raws", bufs=1))
        keep = ctx.enter_context(tc.tile_pool(name="keep", bufs=1))
        work = ctx.enter_context(tc.tile_pool(name="work", bufs=2))
        psum = ctx.enter_context(tc.psum_pool(name="psum", bufs=1))

        live = {}

        def bank(b):
            return psum.tile([P, CHUNK], F32, name="bank%d" % b)

        queued = {"V": 0, "S": 0}

        def count(eng, elements):
            queued[eng] = queued[eng] + elements

        def idler():
            return "V" if queued["V"] <= queued["S"] else "S"

        def copy_out(dst, src, eng=None, elements=CHUNK):
            eng = eng or idler()
            count(eng, elements)
            if eng == "V":
                nc.vector.tensor_copy(out=dst, in_=src)
            else:
                nc.scalar.copy(out=dst, in_=src)

        xis_bf = const.tile([P, PASSES, PACK], BF16, name="xis_bf")
        nc.scalar.dma_start(out=xis_bf[:], in_=xis.rearrange("(c p j) -> p c j", c=PASSES, p=P, j=PACK))
        proj_raw = []
        chunk_raw = []

        for c in range(PASSES):
            proj_raw.append(raws.tile([P, PACK * D], BF16, name="proj_raw%d" % c))
        for k in range(CHUNKS):
            chunk_raw.append(raws.tile([P, ROWS * D], BF16, name="chunk_raw%d" % k))

        def load_proj(c, j, rows):
            src = proj_matrix[c * CHUNK : (c + 1) * CHUNK, :].rearrange("(p j) d -> p j d", j=PACK)
            dst = proj_raw[c][:].rearrange("p (j d) -> p j d", j=PACK)
            nc.sync.dma_start(out=dst[:, j : j + rows, :], in_=src[:, j : j + rows, :])

        def load_chunk(k, n, groups):
            kind, m = SEQ[k]
            if kind == "w":
                src = input_weights[m * CHUNK : (m + 1) * CHUNK, :].rearrange("(n p) d -> p n d", p=P)
            else:
                src = x_rows[m * CHUNK : (m + 1) * CHUNK, :].rearrange("(p n) d -> p n d", n=ROWS)
            dst = chunk_raw[k][:].rearrange("p (n d) -> p n d", n=ROWS)
            nc.sync.dma_start(out=dst[:, n : n + groups, :], in_=src[:, n : n + groups, :])

        for n in range(ROWS):
            load_proj(0, n, 1)
            load_chunk(0, n, 1)
        load_proj(1, 0, PACK)
        for k in range(1, CHUNKS):
            load_chunk(k, 0, ROWS)

        zeros = const.tile([P, CHUNK], BF16, name="zeros")
        nc.gpsimd.memset(zeros[:].bitcast(F32), 0.0)
        ident = const.tile([P, P], F32, name="ident")
        make_identity(nc, ident[:])
        warm = const.tile([P, 1], F32, name="warm")
        nc.vector.memset(warm[:], 0.0)
        nc.scalar.activation(out=warm[:], in_=warm[:], func=ACT.Exp)
        def keep_warm(b, times):
            for rep in range(times):
                nc.tensor.matmul(out=bank(b)[:], lhsT=zeros[:, 0:P], rhs=zeros[:], start=True, stop=True)

        keep_warm(BANKS - 1, WARM_UP)
        xis32 = const.tile([P, PER_CHUNK], F32, name="xis32")
        nc.vector.tensor_copy(out=xis32[:], in_=xis_bf[:].rearrange("p c j -> p (c j)"))
        neg_half_sq = const.tile([P, PER_CHUNK], F32, name="neg_half_sq")
        nc.vector.scalar_tensor_tensor(
            out=neg_half_sq[:], in0=xis32[:], scalar=-0.5, in1=xis32[:], op0=ALU.mult, op1=ALU.mult
        )
        exp_bias = const.tile([P, PER_CHUNK], F32, name="exp_bias")
        nc.vector.tensor_scalar_add(out=exp_bias[:], in0=xis32[:], scalar1=-math.log(32.0))

        g_grouped = keep.tile([P, PASSES * PASSES * CHUNK * PACK], BF16, name="g_grouped", align_bytes=64)
        g_codes = keep.tile([P, PASSES * PASSES * CHUNK], U32, name="g_codes", align_bytes=64)
        g_scales = keep.tile([P, PASSES * PASSES * CHUNK], U8, name="g_scales", align_bytes=64)
        w_codes = keep.tile([P, PASSES * O], U32, name="w_codes", align_bytes=64)
        w_scales = keep.tile([P, PASSES * O], U8, name="w_scales", align_bytes=64)
        squares = keep.tile([P, D], BF16, name="squares")

        def word_transposes(rows, n, b):
            words = rows[:].bitcast(F32)
            ps = bank(b)
            for v in range(4):
                lo = (D // 2) * n + P * v
                nc.tensor.transpose(ps[:, P * v : P * (v + 1)], words[:, lo : lo + P], ident[:])
            return ps

        g_rows = [raws.tile([P, PACK * D], BF16, name="g_rows%d" % c) for c in range(PASSES)]

        def g_scale(c, j):
            cols = slice(j * D, (j + 1) * D)
            cj = PACK * c + j
            count("V", D // 4)
            nc.vector.tensor_scalar_mul(out=g_rows[c][:, cols], in0=proj_raw[c][:, cols], scalar1=xis32[:, cj : cj + 1])

        def g_transposes(c, j, b):
            live[("g", c, j)] = word_transposes(g_rows[c], j, b)

        def g_out(c, j, eng=None):
            words = g_grouped[:].bitcast(F32).rearrange("q (b t u) -> q b t u", b=PASSES * PASSES, u=2)
            copy_out(
                words[:, c * PASSES : (c + 1) * PASSES, j * P : (j + 1) * P, :],
                live[("g", c, j)][:].rearrange("q (a u t) -> q a t u", a=PASSES, u=2),
                eng,
            )

        def g_quantise(c):
            lo = c * PASSES * CHUNK
            width = PASSES * CHUNK
            count("V", width)
            nc.vector.quantize_mx(
                out=g_codes[:, lo : lo + width].bitcast(FP8X4),
                scales=g_scales[:, lo : lo + width],
                in_=g_grouped[:, lo * PACK : (lo + width) * PACK],
            )

        def norm(k, n):
            acc = const.tile([P, 1], F32, name="norm%d_%d" % (k, n))
            count("S", D)
            nc.scalar.activation(
                out=squares[:], in_=chunk_raw[k][:, n * D : (n + 1) * D], func=ACT.Square, accum_out=acc[:]
            )
            live[("norm", k, n)] = acc

        def transposes(k, n, b):
            live[("transposed", k, n)] = word_transposes(chunk_raw[k], n, b)

        def transposes_out(k, n):
            if n == 0:
                live[("grouped", k)] = work.tile([P, PASSES * CHUNK * PACK], BF16, name="grouped", align_bytes=64)
            words = live[("grouped", k)][:].bitcast(F32).rearrange("q (a t u) -> q a t u", a=PASSES, u=2)
            copy_out(
                words[:, :, n * P : (n + 1) * P, :],
                live[("transposed", k, n)][:].rearrange("q (a u t) -> q a t u", a=PASSES, u=2),
            )

        def quantise_input(k):
            codes = work.tile([P, PASSES * CHUNK], U32, name="in_codes", align_bytes=64)
            scales = work.tile([P, PASSES * CHUNK], U8, name="in_scales", align_bytes=64)
            count("V", PASSES * CHUNK)
            nc.vector.quantize_mx(out=codes[:].bitcast(FP8X4), scales=scales[:], in_=live[("grouped", k)][:])
            live[("in", k)] = (codes, scales)

        def spread_norms(k, b):
            ps = bank(b)
            for n in range(ROWS):
                nc.tensor.transpose(
                    ps[:, n * P : (n + 1) * P], live[("norm", k, n)][:, 0:1].to_broadcast([P, P]), ident[:]
                )
            live[("spread", k)] = ps

        def spread_norms_out(k, eng=None):
            row = work.tile([P, CHUNK], F32, name="norm_row", bufs=3)
            copy_out(row[:], live[("spread", k)][:], eng)
            live[("row", k)] = row

        rounds = [(k, c, 0, CHUNK) for k in range(CHUNKS) for c in range(PASSES)]
        rounds[-1:] = [(CHUNKS - 1, 1, 0, CHUNK // 2), (CHUNKS - 1, 1, CHUNK // 2, CHUNK // 2)]
        n_banks1 = PACK * len(rounds)
        gpsimd_rounds = len(rounds) - 2

        def first_stage(i):
            rd, j = divmod(i, PACK)
            k, c, t0, wid = rounds[rd]
            codes, scales = live[("in", k)]
            ps = bank(S1_BANKS[i % len(S1_BANKS)])
            for a in range(PASSES):
                lo = (c * PASSES + a) * CHUNK + j * P
                nc.tensor.matmul_mx(
                    out=ps[:, 0:wid],
                    lhsT=g_codes[:, lo : lo + P].bitcast(FP8X4),
                    lhsT_scale=g_scales[:, lo : lo + P],
                    rhs=codes[:, a * CHUNK + t0 : a * CHUNK + t0 + wid].bitcast(FP8X4),
                    rhs_scale=scales[:, a * CHUNK + t0 : a * CHUNK + t0 + wid],
                    start=(a == 0),
                    stop=(a == PASSES - 1),
                )
            live[("dot", i)] = ps

        def correct(i):
            rd, j = divmod(i, PACK)
            k, c, t0, wid = rounds[rd]
            cj = PACK * c + j
            exponent = work.tile([P, CHUNK], F32, name="exponent", bufs=EXP_LAG + 2)
            count("V", wid)
            nc.vector.scalar_tensor_tensor(
                out=exponent[:, 0:wid],
                in0=live[("row", k)][:, t0 : t0 + wid],
                scalar=neg_half_sq[:, cj : cj + 1],
                in1=live[("dot", i)][:, 0:wid],
                op0=ALU.mult,
                op1=ALU.add,
            )
            live[("exponent", i)] = exponent

        def exponential(i):
            rd, j = divmod(i, PACK)
            k, c, t0, wid = rounds[rd]
            cj = PACK * c + j
            count("S", wid)
            if j == 0:
                live[("planes", rd)] = work.tile([P, PACK, CHUNK], BF16, name="planes")
            nc.scalar.activation(
                out=live[("planes", rd)][:, j, 0:wid],
                in_=live[("exponent", i)][:, 0:wid],
                func=ACT.Exp,
                bias=exp_bias[:, cj : cj + 1],
                scale=1.0,
            )

        def interleave(rd):
            k, c, t0, wid = rounds[rd]
            side = work.tile([P, CHUNK * PACK], BF16, name="side", bufs=1, align_bytes=64)
            planes = live[("planes", rd)]
            if rd < gpsimd_rounds:
                nc.gpsimd.tensor_scalar(
                    out=side[:, 0 : wid * PACK].rearrange("p (t j) -> p t j", j=PACK),
                    in0=planes[:, :, 0:wid].rearrange("p j t -> p t j"),
                    scalar1=1.0,
                    scalar2=0.0,
                    op0=ALU.mult,
                    op1=ALU.add,
                )
            else:
                count("V", 2 * wid)
                nc.vector.tensor_copy(
                    out=side[:, 0 : wid * PACK].rearrange("p (l f j) -> p l j f", f=4, j=PACK),
                    in_=planes[:, :, 0:wid].rearrange("p j (l f) -> p l j f", f=4),
                )
            live[("side", rd)] = side

        def quantise_round(rd):
            k, c, t0, wid = rounds[rd]
            count("V", wid)
            kind, m = SEQ[k]
            if kind == "w":
                codes, scales, lo = w_codes, w_scales, c * O + m * CHUNK
            else:
                if c == 0:
                    live[("feats", m)] = (
                        work.tile([P, PASSES * CHUNK], U32, name="f_codes", align_bytes=64),
                        work.tile([P, PASSES * CHUNK], U8, name="f_scales", align_bytes=64),
                    )
                codes, scales = live[("feats", m)]
                lo = c * CHUNK + t0
            nc.vector.quantize_mx(
                out=codes[:, lo : lo + wid].bitcast(FP8X4),
                scales=scales[:, lo : lo + wid],
                in_=live[("side", rd)][:, 0 : wid * PACK],
            )

        items = []
        ticks2 = {}

        def plan(position, found):
            start = PER_CHUNK * (position + 1) + EXP_LAG + QUANT_LAG
            for n, item in enumerate(found):
                ticks2[start + n] = len(items)
                items.append(item)

        plan(1, [(0, n, 0, CHUNK) for n in range(ROWS)])
        plan(2, [(0, n, CHUNK, CHUNK) for n in range(ROWS)])
        for m in range(1, T // CHUNK):
            plan(m + 2, [(m, n, first, CHUNK) for n in range(ROWS) for first in (0, CHUNK)])
        n_banks2 = len(items)
        last_banks2 = PER_CHUNK // 2

        def second_stage(item, b):
            m, n, first, width = item
            codes, scales = live[("feats", m)]
            ps = bank(b)
            for c in range(PASSES):
                lo = c * CHUNK + n * P
                wlo = c * O + first
                nc.tensor.matmul_mx(
                    out=ps[:, 0:width],
                    lhsT=codes[:, lo : lo + P].bitcast(FP8X4),
                    lhsT_scale=scales[:, lo : lo + P],
                    rhs=w_codes[:, wlo : wlo + width].bitcast(FP8X4),
                    rhs_scale=w_scales[:, wlo : wlo + width],
                    start=(c == 0),
                    stop=(c == PASSES - 1),
                )
            live[("out", item)] = ps

        def second_stage_out(item):
            m, n, first, width = item
            if first == 0:
                live[("staged", m, n)] = work.tile([P, O], F32, name="staged", bufs=8)
            staged = live[("staged", m, n)]
            cols = slice(first, first + width)
            copy_out(staged[:, cols], live[("out", item)][:, 0:width], elements=width)
            dst = out_rows[m * CHUNK : (m + 1) * CHUNK, :].rearrange("(p n) o -> p n o", n=ROWS)
            if m >= BANKWISE_STORES:
                nc.sync.dma_start(out=dst[:, n, cols], in_=staged[:, cols])
            elif first + width == O:
                nc.sync.dma_start(out=dst[:, n, :], in_=staged[:])

        for n in range(ROWS + 1):
            if n < ROWS:
                g_scale(0, n)
                g_transposes(0, n, n)
                transposes(0, n, ROWS + n)
                keep_warm(BANKS - 1 if n < ROWS - 1 else S1_BANKS[0], 2)
                norm(0, n)
            if n > 0:
                g_out(0, n - 1)
                transposes_out(0, n - 1)
        spread_norms(0, ROWS)
        spread_norms_out(0, "S")
        def g1(j):
            g_scale(1, j)
            g_transposes(1, j, G1_BANKS[j])

        g1(0)
        g1(1)
        keep_warm(S1_BANKS[2], 2)
        g_quantise(0)
        g1(2)
        g1(3)
        quantise_input(0)
        transposes(1, 0, T_BANKS[0])
        keep_warm(S1_BANKS[2], 2)
        g_out(1, 0, "S")
        g_out(1, 1, "S")
        norm(1, 0)
        g_out(1, 2, "S")
        g_out(1, 3, "S")
        transposes_out(1, 0)

        def due(what, i):
            found = []
            for k in range(1, CHUNKS):
                for offset, groups in FRONT[what].items():
                    if max(PER_CHUNK * k + offset, -1) == i:
                        found.extend((k, n) for n in groups)
            return found

        out_next = None
        for i in range(-LEAD, max(ticks2) + 1 - last_banks2):
            s = ticks2.get(i)
            fresh = s is not None and s % PER_CHUNK == 0
            if s is not None and not fresh:
                second_stage(items[s], S2_BANKS[s % len(S2_BANKS)])
            if i < min(ticks2) and due("quantise", i - 2):
                keep_warm(S2_BANKS[0], 1)
            if i + LEAD < n_banks1:
                first_stage(i + LEAD)
            if fresh:
                second_stage(items[s], S2_BANKS[s % len(S2_BANKS)])
            for k, n in due("turn", i):
                if (k, n) != (1, 0):
                    transposes(k, n, T_BANKS[n % 2])
            for k, n in due("spread", i):
                spread_norms(k, T_BANKS[0])
            if 0 <= i < n_banks1:
                correct(i)
            if i == 1:
                g_quantise(1)
            if 0 <= i - EXP_LAG < n_banks1:
                exponential(i - EXP_LAG)
            rd, rest = divmod(i - EXP_LAG - (PACK - 1), PACK)
            if rest == 0 and 0 <= rd < gpsimd_rounds:
                interleave(rd)
            rd, rest = divmod(i - EXP_LAG - (PACK - 1) - 1, PACK)
            if rest == 0 and gpsimd_rounds <= rd < len(rounds):
                interleave(rd)
            rd, rest = divmod(i - EXP_LAG - (PACK - 1) - 2, PACK)
            if rest == 0 and gpsimd_rounds <= rd < len(rounds):
                quantise_round(rd)
            rd, rest = divmod(i - EXP_LAG - (PACK - 1) - QUANT_LAG, PACK)
            if rest == 0 and 0 <= rd < gpsimd_rounds:
                quantise_round(rd)
            for k, n in due("quantise", i):
                quantise_input(k)
            for k, n in due("turn_out", i):
                if (k, n) != (1, 0):
                    transposes_out(k, n)
            for k, n in due("spread_out", i):
                spread_norms_out(k)
            if out_next is not None:
                second_stage_out(items[out_next])
            out_next = s
            for k, n in due("norm", i):
                if (k, n) != (1, 0):
                    norm(k, n)

        second_stage_out(items[n_banks2 - last_banks2 - 1])
        end_items = items[n_banks2 - last_banks2 :]
        m, n, first, width = end_items.pop()
        end_items.extend((m, n, first + e * width // 2, width // 2) for e in range(2))
        end_banks = T_BANKS + S1_BANKS
        for item, b in zip(end_items, end_banks):
            second_stage(item, b)
        for item in end_items:
            second_stage_out(item)
